import numpy as np
import ml_dtypes


def mxq(x, axis, fmt="e4m3"):
    dtype, down = {"e4m3": (ml_dtypes.float8_e4m3fn, 7), "e5m2": (ml_dtypes.float8_e5m2, 14)}[fmt]
    v = np.moveaxis(np.asarray(x, np.float32).astype(ml_dtypes.bfloat16).astype(np.float64), axis, -1)
    blocks = v.reshape(v.shape[:-1] + (-1, 32))
    amax = np.abs(blocks).max(-1, keepdims=True)
    byte = np.maximum(np.where(amax > 0, np.frexp(amax)[1] - 1 + 127, 0) - down, 1)
    scale = np.exp2(byte - 127.0)
    codes = (blocks / scale).astype(np.float32).astype(dtype).astype(np.float64)
    return np.moveaxis((codes * scale).reshape(v.shape), -1, axis)


WIDE = False


def mx_kscale(k):
    if not WIDE:
        return np.ones(k)
    levels = np.array([10, -10, 5, -5, 0])
    a = np.random.permutation(np.resize(levels, k // 512 * 4)).reshape(k // 512, 4)
    idx = np.arange(k)
    return np.exp2(a[idx // 512, idx % 128 // 32])


BF16 = ml_dtypes.bfloat16


def bf(x):
    return np.asarray(x, np.float32).astype(BF16)


def f64(x):
    return np.asarray(x).astype(np.float64)


E2M1 = np.array([0.0, 0.5, 1.0, 1.5, 2.0, 3.0, 4.0, 6.0, -0.0, -0.5, -1.0, -1.5, -2.0, -3.0, -4.0, -6.0])


def pack_weight(w, fmt):
    k, n = w.shape
    w = f64(bf(w)).reshape(k // 32, 32, n)
    amax = np.abs(w).max(1)
    if fmt == "e4m3":
        byte = np.frexp(amax)[1] - 1 + 127 - 7
    else:
        mant, ex = np.frexp(amax / 6.0)
        byte = np.where(mant > 0.5, ex, ex - 1) + 127
    byte = np.clip(np.where(amax > 0, byte, 1), 1, 254)
    scaled = (w * np.exp2(127.0 - byte)[:, None, :]).reshape(k, n).astype(np.float32)
    by_word = np.ascontiguousarray(scaled.reshape(k // 512, 128, 4, n).transpose(0, 1, 3, 2))
    if fmt == "e4m3":
        words = by_word.astype(ml_dtypes.float8_e4m3fn).view(np.uint8)
    else:
        c = by_word.astype(ml_dtypes.float4_e2m1fn).view(np.uint8) & 0xF
        words = c[..., 0::2] | (c[..., 1::2] << 4)
    return np.ascontiguousarray(words), np.ascontiguousarray(byte.astype(np.uint8).reshape(k // 512, 16, n))


def unpack_weight(words, scales, fmt):
    g, p, n, _ = words.shape
    if fmt == "e4m3":
        vals = np.ascontiguousarray(words).view(ml_dtypes.float8_e4m3fn).astype(np.float64)
    else:
        nib = np.empty((g, p, n, 4), np.uint8)
        nib[..., 0::2] = words & 0xF
        nib[..., 1::2] = words >> 4
        vals = E2M1[nib]
    vals = vals * np.repeat(np.exp2(scales.astype(np.float64) - 127.0), 8, axis=1)[..., None]
    return vals.transpose(0, 1, 3, 2).reshape(g * 512, n)

def pack4(w):
    words, scales = pack_weight(w, "e2m1")
    return words.reshape(words.shape[0], 128, -1), scales


def unpack4(words, scales):
    return unpack_weight(words.reshape(words.shape[0], 128, -1, 2), scales, "e2m1")


B, I, H = 512, 1024, 1024
G = 4
MXH = H % 512 == 0


def sigmoid(v):
    return 1.0 / (1.0 + np.exp(-v))


def setup_inputs():
    s = mx_kscale(I)
    t = mx_kscale(H) if MXH else np.ones(H)
    x = bf(np.random.standard_normal((B, I)) * s)
    h = bf(np.random.standard_normal((B, H)) * t)
    c = bf(np.random.standard_normal((B, H)))
    wx = np.random.standard_normal((G, H, I)) * 0.8 / np.sqrt(I) / s
    cat = np.ascontiguousarray(wx.swapaxes(1, 2)).reshape(-1, H)
    Wx_words, Wx_scales = pack4(cat)
    Wh = bf(np.random.standard_normal((4, H, H)) * 0.8 / np.sqrt(H) / t)
    bx = bf(np.random.standard_normal((4, H)) * 0.3)
    bh = bf(np.random.standard_normal((4, H)) * 0.3)
    return {"x": x, "h": h, "c": c, "Wx_words": Wx_words, "Wx_scales": Wx_scales,
            "Wh": Wh, "bx": bx, "bh": bh}


def reference(x, h, c, Wx_words, Wx_scales, Wh, bx, bh):
    wx = unpack4(Wx_words, Wx_scales).reshape(G, I, H).swapaxes(1, 2).reshape(G * H, I)
    wh = f64(Wh).reshape(4 * H, H)
    gx = (mxq(f64(x), 1, "e4m3") @ wx.T) + f64(bx).reshape(-1)
    if MXH:
        gh = (mxq(f64(h), 1, "e4m3") @ mxq(wh, 1, "e4m3").T) + f64(bh).reshape(-1)
    else:
        gh = f64(h) @ wh.T + f64(bh).reshape(-1)
    g = (gx + gh).reshape(-1, 4, H)
    i = sigmoid(g[:, 0])
    f = sigmoid(g[:, 1])
    gc = np.tanh(g[:, 2])
    o = sigmoid(g[:, 3])
    c_new = f * f64(c) + i * gc
    hs = o * np.tanh(c_new)
    return (hs, c_new)

@@ -1,0 +1,212 @@
+from contextlib import ExitStack
+
+import concourse.mybir as mybir
+from concourse.masks import make_identity
+
+F32 = mybir.dt.float32
+BF16 = mybir.dt.bfloat16
+I32 = mybir.dt.int32
+U32 = mybir.dt.uint32
+U8 = mybir.dt.uint8
+FP8X4 = mybir.dt.float8_e4m3fn_x4
+FP4X4 = mybir.dt.float4_e2m1fn_x4
+SIGMOID = mybir.ActivationFunctionType.Sigmoid
+TANH = mybir.ActivationFunctionType.Tanh
+
+P = 128
+PACK = 4
+K_PASS = P * PACK
+BATCH = 512
+K = 1024
+HIDDEN = 1024
+PASSES = K // K_PASS
+BLOCK_ROWS = 512
+ROW_TILES = BLOCK_ROWS // P
+WORDS = K // 2
+PASS_WORDS = K_PASS // 2
+HALVES = HIDDEN // BLOCK_ROWS
+
+GATE_I, GATE_F, GATE_G, GATE_O = 0, 1, 2, 3
+GATE_ORDER = (GATE_F, GATE_I, GATE_G, GATE_O)
+
+FLOPS = 2 * BATCH * 4 * HIDDEN * 2 * K
+
+
+def tile_lstmcell_e_kernel(tc, x, h, c, Wx_words, Wx_scales, Wh, bx, bh, out_0, out_1):
+    nc = tc.nc
+    blocks = [(half, gate) for half in range(HALVES) for gate in GATE_ORDER]
+
+    with ExitStack() as ctx:
+        keep = ctx.enter_context(tc.tile_pool(name="keep", bufs=1))
+        grouped_pool = ctx.enter_context(tc.tile_pool(name="grouped", bufs=3))
+        wh_mx_pool = ctx.enter_context(tc.tile_pool(name="wh_mx", bufs=3))
+        bias_pool = ctx.enter_context(tc.tile_pool(name="bias", bufs=3))
+        gate_pool = ctx.enter_context(tc.tile_pool(name="gates", bufs=ROW_TILES))
+        flip_psum = ctx.enter_context(tc.psum_pool(name="flip", bufs=4))
+        sum_psum = ctx.enter_context(tc.psum_pool(name="sums", bufs=4))
+        ctx.enter_context(tc.manual_schedule())
+
+        wx_planes = keep.tile([P, 4 * PASSES, HIDDEN], U8, align_bytes=64)
+        nc.vector.memset(wx_planes[:].rearrange("p s n -> p (s n)").bitcast(I32), 0)
+        bias_rows = keep.tile([P, 4 * HIDDEN], BF16)
+        nc.vector.memset(bias_rows[:].bitcast(I32), 0)
+        ones = keep.tile([P, P], BF16)
+        nc.vector.memset(ones[:], 1.0)
+        warm = keep.tile([P, 1], F32)
+        nc.vector.memset(warm[:], 0.0)
+        identity = keep.tile([P, P], F32)
+        make_identity(nc, identity[:])
+        nc.scalar.activation(out=warm[:], in_=warm[:], func=SIGMOID)
+
+        def load_rows(rows, label):
+            raw = keep.tile([P, ROW_TILES, K], BF16, name="raw_" + label, tag="raw_" + label)
+            for r in range(ROW_TILES):
+                nc.sync.dma_start(out=raw[:, r, :], in_=rows[r * P : (r + 1) * P, :])
+            return raw
+
+        x_raw = load_rows(x, "x")
+        h_raw = load_rows(h, "h")
+        nc.sync.dma_start(out=bias_rows[0:1, :], in_=bx.rearrange("(o g) n -> o (g n)", o=1))
+        nc.sync.dma_start(out=bias_rows[1:2, :], in_=bh.rearrange("(o g) n -> o (g n)", o=1))
+
+        wx_words = keep.tile([P, 4 * PASSES, 2 * HIDDEN], U8, align_bytes=64)
+        words_dram = Wx_words.bitcast(I32)
+        scales_dram = Wx_scales.bitcast(I32).rearrange("s (q r) n -> r q s n", r=4)
+        c_sb = keep.tile([P, ROW_TILES, HIDDEN], BF16)
+        wh_raw = []
+        for half in range(HALVES):
+            for gate in GATE_ORDER:
+                wh_rows = Wh[gate, half * BLOCK_ROWS : (half + 1) * BLOCK_ROWS, :]
+                wh_raw.append(load_rows(wh_rows, "wh%d%d" % (half, gate)))
+                if half == 0:
+                    first, last = gate * PASSES, (gate + 1) * PASSES
+                    for r in range(4):
+                        nc.sync.dma_start(
+                            out=wx_planes[r:P:32, first:last, :].bitcast(I32),
+                            in_=scales_dram[r][:, first:last, :],
+                        )
+                    nc.sync.dma_start(
+                        out=wx_words[:, first:last, :].bitcast(I32),
+                        in_=words_dram[first:last].rearrange("s p n -> p s n"),
+                    )
+            if half == 0:
+                nc.sync.dma_start(out=c_sb[:], in_=c.rearrange("(b p) n -> p b n", p=P))
+
+        def transpose_block(raw, k_step, copy_out):
+            grouped = grouped_pool.tile([P, PASSES, BLOCK_ROWS, PACK], BF16, align_bytes=64)
+            for r in range(ROW_TILES):
+                words = raw[:, r, :].bitcast(F32)
+                flipped = flip_psum.tile([P, PASSES, 2, P], F32, tag="bank")
+                for s in range(PASSES):
+                    for u in range(2):
+                        if k_step == 2:
+                            cols = words[:, s * PASS_WORDS + u : (s + 1) * PASS_WORDS : 2]
+                        else:
+                            cols = words[:, s * PASS_WORDS + u * P : s * PASS_WORDS + (u + 1) * P]
+                        nc.tensor.transpose(flipped[:, s, u, :], cols, identity[:])
+                copy_out(
+                    out=grouped[:, :, r * P : (r + 1) * P, :].bitcast(F32),
+                    in_=flipped[:].rearrange("p s u n -> p s n u"),
+                )
+            return grouped
+
+        def quantise(grouped, codes, planes):
+            nc.vector.quantize_mx(
+                out=codes[:].rearrange("p s n -> p (s n)").bitcast(FP8X4),
+                scales=planes[:].rearrange("p s n -> p (s n)"),
+                in_=grouped[:].rearrange("p s n t -> p (s n t)"),
+            )
+
+        x_codes = keep.tile([P, PASSES, BATCH], U32, align_bytes=64)
+        x_planes = keep.tile([P, PASSES, BATCH], U8, align_bytes=64)
+        h_codes = keep.tile([P, PASSES, BATCH], U32, align_bytes=64)
+        h_planes = keep.tile([P, PASSES, BATCH], U8, align_bytes=64)
+        x_grouped = transpose_block(x_raw, 2, nc.vector.tensor_copy)
+        h_grouped = transpose_block(h_raw, 1, nc.vector.tensor_copy)
+        quantise(x_grouped, x_codes, x_planes)
+        quantise(h_grouped, h_codes, h_planes)
+
+        wh_grouped = {}
+        wh_mx = {}
+        bias = {}
+        gates = {}
+
+        def prepare(n):
+            half, gate = blocks[n]
+            wh_grouped[n] = transpose_block(wh_raw[n], 1, nc.scalar.copy)
+            start_col = gate * HIDDEN + half * BLOCK_ROWS
+            spread = flip_psum.tile([P, BLOCK_ROWS], F32, tag="bank")
+            nc.tensor.matmul(
+                spread[:], lhsT=ones[:], rhs=bias_rows[:, start_col : start_col + BLOCK_ROWS], start=True, stop=True
+            )
+            bias[n] = bias_pool.tile([P, BLOCK_ROWS], F32, name="bias_sb")
+            nc.scalar.copy(out=bias[n][:], in_=spread[:])
+
+        def quantise_block(n):
+            codes = wh_mx_pool.tile([P, PASSES, BLOCK_ROWS], U32, name="wh_codes", align_bytes=64)
+            planes = wh_mx_pool.tile([P, PASSES, BLOCK_ROWS], U8, name="wh_planes", align_bytes=64)
+            quantise(wh_grouped[n], codes, planes)
+            wh_mx[n] = (codes, planes)
+
+        def gate_values(n, b):
+            half, gate = blocks[n]
+            wh_codes, wh_planes = wh_mx[n]
+            rows = slice(b * P, (b + 1) * P)
+            acc = sum_psum.tile([P, BLOCK_ROWS], F32)
+            for s in range(PASSES):
+                nc.tensor.matmul_mx(
+                    out=acc[:],
+                    lhsT=x_codes[:, s, rows].bitcast(FP8X4),
+                    lhsT_scale=x_planes[:, s, rows],
+                    rhs=wx_words[
+                        :, gate * PASSES + s, 2 * half * BLOCK_ROWS : 2 * (half + 1) * BLOCK_ROWS
+                    ].bitcast(FP4X4),
+                    rhs_scale=wx_planes[:, gate * PASSES + s, half * BLOCK_ROWS : (half + 1) * BLOCK_ROWS],
+                    start=(s == 0),
+                    stop=False,
+                )
+            for s in range(PASSES):
+                nc.tensor.matmul_mx(
+                    out=acc[:],
+                    lhsT=h_codes[:, s, rows].bitcast(FP8X4),
+                    lhsT_scale=h_planes[:, s, rows],
+                    rhs=wh_codes[:, s, :].bitcast(FP8X4),
+                    rhs_scale=wh_planes[:, s, :],
+                    start=False,
+                    stop=(s == PASSES - 1),
+                )
+            value = gate_pool.tile([P, BLOCK_ROWS], F32, name="gate%d" % gate, tag="gate%d" % gate)
+            nc.vector.tensor_add(out=value[:], in0=acc[:], in1=bias[n][:])
+            nc.scalar.activation(out=value[:], in_=value[:], func=(TANH if gate == GATE_G else SIGMOID))
+            gates[(gate, b)] = value
+
+        def combine(n, b):
+            half, gate = blocks[n]
+            rows = slice(b * P, (b + 1) * P)
+            cols = slice(half * BLOCK_ROWS, (half + 1) * BLOCK_ROWS)
+            f, i, g, o = [gates.get((e, b)) for e in (GATE_F, GATE_I, GATE_G, GATE_O)]
+            if gate == GATE_I:
+                nc.vector.tensor_mul(out=f[:], in0=f[:], in1=c_sb[:, b, cols])
+            if gate == GATE_G:
+                nc.vector.tensor_mul(out=i[:], in0=i[:], in1=g[:])
+                nc.vector.tensor_add(out=f[:], in0=f[:], in1=i[:])
+                nc.sync.dma_start(out=out_1[rows, cols], in_=f[:])
+                nc.scalar.activation(out=g[:], in_=f[:], func=TANH)
+            if gate == GATE_O:
+                nc.vector.tensor_mul(out=o[:], in0=o[:], in1=g[:])
+                nc.sync.dma_start(out=out_0[rows, cols], in_=o[:])
+
+        prepare(0)
+        prepare(1)
+        quantise_block(0)
+        for n in range(len(blocks)):
+            if n + 1 < len(blocks):
+                quantise_block(n + 1)
+            for b in range(ROW_TILES):
+                gate_values(n, b)
+                if n >= 1:
+                    combine(n - 1, b)
+            if n + 2 < len(blocks):
+                prepare(n + 2)
+        for b in range(ROW_TILES):
+            combine(len(blocks) - 1, b)

@@ -25,6 +25,7 @@ ROW_TILES = BLOCK_ROWS // P
 WORDS = K // 2
 PASS_WORDS = K_PASS // 2
 HALVES = HIDDEN // BLOCK_ROWS
+WH_SCALAR_TILES = 3
 
 GATE_I, GATE_F, GATE_G, GATE_O = 0, 1, 2, 3
 GATE_ORDER = (GATE_F, GATE_I, GATE_G, GATE_O)
@@ -92,7 +93,7 @@ def tile_lstmcell_e_kernel(tc, x, h, c, Wx_words, Wx_scales, Wh, bx, bh, out_0, 
             if half == 0:
                 nc.sync.dma_start(out=c_sb[:], in_=c.rearrange("(b p) n -> p b n", p=P))
 
-        def transpose_block(raw, k_step, copy_out):
+        def transpose_block(raw, k_step, scalar_tiles):
             grouped = grouped_pool.tile([P, PASSES, BLOCK_ROWS, PACK], BF16, align_bytes=64)
             for r in range(ROW_TILES):
                 words = raw[:, r, :].bitcast(F32)
@@ -104,6 +105,7 @@ def tile_lstmcell_e_kernel(tc, x, h, c, Wx_words, Wx_scales, Wh, bx, bh, out_0, 
                         else:
                             cols = words[:, s * PASS_WORDS + u * P : s * PASS_WORDS + (u + 1) * P]
                         nc.tensor.transpose(flipped[:, s, u, :], cols, identity[:])
+                copy_out = nc.scalar.copy if r < scalar_tiles else nc.vector.tensor_copy
                 copy_out(
                     out=grouped[:, :, r * P : (r + 1) * P, :].bitcast(F32),
                     in_=flipped[:].rearrange("p s u n -> p s n u"),
@@ -121,8 +123,8 @@ def tile_lstmcell_e_kernel(tc, x, h, c, Wx_words, Wx_scales, Wh, bx, bh, out_0, 
         x_planes = keep.tile([P, PASSES, BATCH], U8, align_bytes=64)
         h_codes = keep.tile([P, PASSES, BATCH], U32, align_bytes=64)
         h_planes = keep.tile([P, PASSES, BATCH], U8, align_bytes=64)
-        x_grouped = transpose_block(x_raw, 2, nc.vector.tensor_copy)
-        h_grouped = transpose_block(h_raw, 1, nc.vector.tensor_copy)
+        x_grouped = transpose_block(x_raw, 2, 0)
+        h_grouped = transpose_block(h_raw, 1, 0)
         quantise(x_grouped, x_codes, x_planes)
         quantise(h_grouped, h_codes, h_planes)
 
@@ -133,9 +135,9 @@ def tile_lstmcell_e_kernel(tc, x, h, c, Wx_words, Wx_scales, Wh, bx, bh, out_0, 
 
         def prepare(n):
             half, gate = blocks[n]
-            wh_grouped[n] = transpose_block(wh_raw[n], 1, nc.scalar.copy)
+            wh_grouped[n] = transpose_block(wh_raw[n], 1, WH_SCALAR_TILES)
             start_col = gate * HIDDEN + half * BLOCK_ROWS
-            spread = flip_psum.tile([P, BLOCK_ROWS], F32, tag="bank")
+            spread = sum_psum.tile([P, BLOCK_ROWS], F32, tag="acc")
             nc.tensor.matmul(
                 spread[:], lhsT=ones[:], rhs=bias_rows[:, start_col : start_col + BLOCK_ROWS], start=True, stop=True
             )
@@ -152,7 +154,7 @@ def tile_lstmcell_e_kernel(tc, x, h, c, Wx_words, Wx_scales, Wh, bx, bh, out_0, 
             half, gate = blocks[n]
             wh_codes, wh_planes = wh_mx[n]
             rows = slice(b * P, (b + 1) * P)
-            acc = sum_psum.tile([P, BLOCK_ROWS], F32)
+            acc = sum_psum.tile([P, BLOCK_ROWS], F32, tag="acc")
             for s in range(PASSES):
                 nc.tensor.matmul_mx(
                     out=acc[:],
@@ -179,34 +181,35 @@ def tile_lstmcell_e_kernel(tc, x, h, c, Wx_words, Wx_scales, Wh, bx, bh, out_0, 
             nc.vector.tensor_add(out=value[:], in0=acc[:], in1=bias[n][:])
             nc.scalar.activation(out=value[:], in_=value[:], func=(TANH if gate == GATE_G else SIGMOID))
             gates[(gate, b)] = value
-
-        def combine(n, b):
-            half, gate = blocks[n]
-            rows = slice(b * P, (b + 1) * P)
+            f, i, g = [gates.get((e, b)) for e in (GATE_F, GATE_I, GATE_G)]
             cols = slice(half * BLOCK_ROWS, (half + 1) * BLOCK_ROWS)
-            f, i, g, o = [gates.get((e, b)) for e in (GATE_F, GATE_I, GATE_G, GATE_O)]
-            if gate == GATE_I:
-                nc.vector.tensor_mul(out=f[:], in0=f[:], in1=c_sb[:, b, cols])
+            if gate == GATE_F:
+                nc.gpsimd.tensor_mul(out=f[:], in0=f[:], in1=c_sb[:, b, cols])
             if gate == GATE_G:
-                nc.vector.tensor_mul(out=i[:], in0=i[:], in1=g[:])
-                nc.vector.tensor_add(out=f[:], in0=f[:], in1=i[:])
+                nc.gpsimd.tensor_mul(out=i[:], in0=i[:], in1=g[:])
+                nc.gpsimd.tensor_add(out=f[:], in0=f[:], in1=i[:])
                 nc.sync.dma_start(out=out_1[rows, cols], in_=f[:])
-                nc.scalar.activation(out=g[:], in_=f[:], func=TANH)
             if gate == GATE_O:
-                nc.vector.tensor_mul(out=o[:], in0=o[:], in1=g[:])
-                nc.sync.dma_start(out=out_0[rows, cols], in_=o[:])
+                nc.scalar.activation(out=g[:], in_=f[:], func=TANH)
+
+        def hidden_state(half, b):
+            o, tanh_c = gates[(GATE_O, b)], gates[(GATE_G, b)]
+            nc.vector.tensor_mul(out=o[:], in0=o[:], in1=tanh_c[:])
+            nc.sync.dma_start(
+                out=out_0[b * P : (b + 1) * P, half * BLOCK_ROWS : (half + 1) * BLOCK_ROWS], in_=o[:]
+            )
 
         prepare(0)
-        prepare(1)
         quantise_block(0)
         for n in range(len(blocks)):
+            half, gate = blocks[n]
             if n + 1 < len(blocks):
-                quantise_block(n + 1)
+                prepare(n + 1)
             for b in range(ROW_TILES):
                 gate_values(n, b)
-                if n >= 1:
-                    combine(n - 1, b)
-            if n + 2 < len(blocks):
-                prepare(n + 2)
-        for b in range(ROW_TILES):
-            combine(len(blocks) - 1, b)
+                if b == 0 and n + 1 < len(blocks):
+                    quantise_block(n + 1)
+                if gate == GATE_O and b >= 1:
+                    hidden_state(half, b - 1)
+            if gate == GATE_O:
+                hidden_state(half, ROW_TILES - 1)

@@ -25,7 +25,6 @@ ROW_TILES = BLOCK_ROWS // P
 WORDS = K // 2
 PASS_WORDS = K_PASS // 2
 HALVES = HIDDEN // BLOCK_ROWS
-WH_SCALAR_TILES = 3
 
 GATE_I, GATE_F, GATE_G, GATE_O = 0, 1, 2, 3
 GATE_ORDER = (GATE_F, GATE_I, GATE_G, GATE_O)
@@ -43,8 +42,9 @@ def tile_lstmcell_e_kernel(tc, x, h, c, Wx_words, Wx_scales, Wh, bx, bh, out_0, 
         wh_mx_pool = ctx.enter_context(tc.tile_pool(name="wh_mx", bufs=3))
         bias_pool = ctx.enter_context(tc.tile_pool(name="bias", bufs=3))
         gate_pool = ctx.enter_context(tc.tile_pool(name="gates", bufs=ROW_TILES))
-        flip_psum = ctx.enter_context(tc.psum_pool(name="flip", bufs=4))
-        sum_psum = ctx.enter_context(tc.psum_pool(name="sums", bufs=4))
+        flip_psum = ctx.enter_context(tc.psum_pool(name="flip", bufs=3))
+        sum_psum = ctx.enter_context(tc.psum_pool(name="sums", bufs=ROW_TILES))
+        spread_psum = ctx.enter_context(tc.psum_pool(name="spread", bufs=1))
         ctx.enter_context(tc.manual_schedule())
 
         wx_planes = keep.tile([P, 4 * PASSES, HIDDEN], U8, align_bytes=64)
@@ -61,14 +61,13 @@ def tile_lstmcell_e_kernel(tc, x, h, c, Wx_words, Wx_scales, Wh, bx, bh, out_0, 
 
         def load_rows(rows, label):
             raw = keep.tile([P, ROW_TILES, K], BF16, name="raw_" + label, tag="raw_" + label)
-            for r in range(ROW_TILES):
-                nc.sync.dma_start(out=raw[:, r, :], in_=rows[r * P : (r + 1) * P, :])
+            nc.sync.dma_start(out=raw[:], in_=rows.rearrange("(r p) k -> p r k", p=P))
             return raw
 
         x_raw = load_rows(x, "x")
         h_raw = load_rows(h, "h")
-        nc.sync.dma_start(out=bias_rows[0:1, :], in_=bx.rearrange("(o g) n -> o (g n)", o=1))
-        nc.sync.dma_start(out=bias_rows[1:2, :], in_=bh.rearrange("(o g) n -> o (g n)", o=1))
+        nc.gpsimd.dma_start(out=bias_rows[0:1, :], in_=bx.rearrange("(o g) n -> o (g n)", o=1))
+        nc.gpsimd.dma_start(out=bias_rows[1:2, :], in_=bh.rearrange("(o g) n -> o (g n)", o=1))
 
         wx_words = keep.tile([P, 4 * PASSES, 2 * HIDDEN], U8, align_bytes=64)
         words_dram = Wx_words.bitcast(I32)
@@ -79,13 +78,11 @@ def tile_lstmcell_e_kernel(tc, x, h, c, Wx_words, Wx_scales, Wh, bx, bh, out_0, 
             for gate in GATE_ORDER:
                 wh_rows = Wh[gate, half * BLOCK_ROWS : (half + 1) * BLOCK_ROWS, :]
                 wh_raw.append(load_rows(wh_rows, "wh%d%d" % (half, gate)))
+                if half == 0 and gate == GATE_ORDER[0]:
+                    for r in range(4):
+                        nc.sync.dma_start(out=wx_planes[r:P:32, :, :].bitcast(I32), in_=scales_dram[r])
                 if half == 0:
                     first, last = gate * PASSES, (gate + 1) * PASSES
-                    for r in range(4):
-                        nc.sync.dma_start(
-                            out=wx_planes[r:P:32, first:last, :].bitcast(I32),
-                            in_=scales_dram[r][:, first:last, :],
-                        )
                     nc.sync.dma_start(
                         out=wx_words[:, first:last, :].bitcast(I32),
                         in_=words_dram[first:last].rearrange("s p n -> p s n"),
@@ -93,7 +90,7 @@ def tile_lstmcell_e_kernel(tc, x, h, c, Wx_words, Wx_scales, Wh, bx, bh, out_0, 
             if half == 0:
                 nc.sync.dma_start(out=c_sb[:], in_=c.rearrange("(b p) n -> p b n", p=P))
 
-        def transpose_block(raw, k_step, scalar_tiles):
+        def transpose_block(raw, k_step, copy_out):
             grouped = grouped_pool.tile([P, PASSES, BLOCK_ROWS, PACK], BF16, align_bytes=64)
             for r in range(ROW_TILES):
                 words = raw[:, r, :].bitcast(F32)
@@ -105,7 +102,6 @@ def tile_lstmcell_e_kernel(tc, x, h, c, Wx_words, Wx_scales, Wh, bx, bh, out_0, 
                         else:
                             cols = words[:, s * PASS_WORDS + u * P : s * PASS_WORDS + (u + 1) * P]
                         nc.tensor.transpose(flipped[:, s, u, :], cols, identity[:])
-                copy_out = nc.scalar.copy if r < scalar_tiles else nc.vector.tensor_copy
                 copy_out(
                     out=grouped[:, :, r * P : (r + 1) * P, :].bitcast(F32),
                     in_=flipped[:].rearrange("p s u n -> p s n u"),
@@ -123,8 +119,8 @@ def tile_lstmcell_e_kernel(tc, x, h, c, Wx_words, Wx_scales, Wh, bx, bh, out_0, 
         x_planes = keep.tile([P, PASSES, BATCH], U8, align_bytes=64)
         h_codes = keep.tile([P, PASSES, BATCH], U32, align_bytes=64)
         h_planes = keep.tile([P, PASSES, BATCH], U8, align_bytes=64)
-        x_grouped = transpose_block(x_raw, 2, 0)
-        h_grouped = transpose_block(h_raw, 1, 0)
+        x_grouped = transpose_block(x_raw, 2, nc.vector.tensor_copy)
+        h_grouped = transpose_block(h_raw, 1, nc.vector.tensor_copy)
         quantise(x_grouped, x_codes, x_planes)
         quantise(h_grouped, h_codes, h_planes)
 
@@ -135,9 +131,9 @@ def tile_lstmcell_e_kernel(tc, x, h, c, Wx_words, Wx_scales, Wh, bx, bh, out_0, 
 
         def prepare(n):
             half, gate = blocks[n]
-            wh_grouped[n] = transpose_block(wh_raw[n], 1, WH_SCALAR_TILES)
+            wh_grouped[n] = transpose_block(wh_raw[n], 1, nc.scalar.copy)
             start_col = gate * HIDDEN + half * BLOCK_ROWS
-            spread = sum_psum.tile([P, BLOCK_ROWS], F32, tag="acc")
+            spread = spread_psum.tile([P, BLOCK_ROWS], F32)
             nc.tensor.matmul(
                 spread[:], lhsT=ones[:], rhs=bias_rows[:, start_col : start_col + BLOCK_ROWS], start=True, stop=True
             )
@@ -150,66 +146,70 @@ def tile_lstmcell_e_kernel(tc, x, h, c, Wx_words, Wx_scales, Wh, bx, bh, out_0, 
             quantise(wh_grouped[n], codes, planes)
             wh_mx[n] = (codes, planes)
 
-        def gate_values(n, b):
+        def x_passes(n):
+            half, gate = blocks[n]
+            for b in range(ROW_TILES):
+                sums[b] = sum_psum.tile([P, BLOCK_ROWS], F32, name="acc")
+                for s in range(PASSES):
+                    nc.tensor.matmul_mx(
+                        out=sums[b][:],
+                        lhsT=x_codes[:, s, b * P : (b + 1) * P].bitcast(FP8X4),
+                        lhsT_scale=x_planes[:, s, b * P : (b + 1) * P],
+                        rhs=wx_words[
+                            :, gate * PASSES + s, 2 * half * BLOCK_ROWS : 2 * (half + 1) * BLOCK_ROWS
+                        ].bitcast(FP4X4),
+                        rhs_scale=wx_planes[:, gate * PASSES + s, half * BLOCK_ROWS : (half + 1) * BLOCK_ROWS],
+                        start=(s == 0),
+                        stop=False,
+                    )
+
+        def h_passes(n, b):
             half, gate = blocks[n]
             wh_codes, wh_planes = wh_mx[n]
-            rows = slice(b * P, (b + 1) * P)
-            acc = sum_psum.tile([P, BLOCK_ROWS], F32, tag="acc")
             for s in range(PASSES):
                 nc.tensor.matmul_mx(
-                    out=acc[:],
-                    lhsT=x_codes[:, s, rows].bitcast(FP8X4),
-                    lhsT_scale=x_planes[:, s, rows],
-                    rhs=wx_words[
-                        :, gate * PASSES + s, 2 * half * BLOCK_ROWS : 2 * (half + 1) * BLOCK_ROWS
-                    ].bitcast(FP4X4),
-                    rhs_scale=wx_planes[:, gate * PASSES + s, half * BLOCK_ROWS : (half + 1) * BLOCK_ROWS],
-                    start=(s == 0),
-                    stop=False,
-                )
-            for s in range(PASSES):
-                nc.tensor.matmul_mx(
-                    out=acc[:],
-                    lhsT=h_codes[:, s, rows].bitcast(FP8X4),
-                    lhsT_scale=h_planes[:, s, rows],
+                    out=sums[b][:],
+                    lhsT=h_codes[:, s, b * P : (b + 1) * P].bitcast(FP8X4),
+                    lhsT_scale=h_planes[:, s, b * P : (b + 1) * P],
                     rhs=wh_codes[:, s, :].bitcast(FP8X4),
                     rhs_scale=wh_planes[:, s, :],
                     start=False,
                     stop=(s == PASSES - 1),
                 )
             value = gate_pool.tile([P, BLOCK_ROWS], F32, name="gate%d" % gate, tag="gate%d" % gate)
-            nc.vector.tensor_add(out=value[:], in0=acc[:], in1=bias[n][:])
+            nc.vector.tensor_add(out=value[:], in0=sums[b][:], in1=bias[n][:])
             nc.scalar.activation(out=value[:], in_=value[:], func=(TANH if gate == GATE_G else SIGMOID))
             gates[(gate, b)] = value
-            f, i, g = [gates.get((e, b)) for e in (GATE_F, GATE_I, GATE_G)]
-            cols = slice(half * BLOCK_ROWS, (half + 1) * BLOCK_ROWS)
-            if gate == GATE_F:
-                nc.gpsimd.tensor_mul(out=f[:], in0=f[:], in1=c_sb[:, b, cols])
-            if gate == GATE_G:
-                nc.gpsimd.tensor_mul(out=i[:], in0=i[:], in1=g[:])
-                nc.gpsimd.tensor_add(out=f[:], in0=f[:], in1=i[:])
-                nc.sync.dma_start(out=out_1[rows, cols], in_=f[:])
-            if gate == GATE_O:
-                nc.scalar.activation(out=g[:], in_=f[:], func=TANH)
 
-        def hidden_state(half, b):
-            o, tanh_c = gates[(GATE_O, b)], gates[(GATE_G, b)]
-            nc.vector.tensor_mul(out=o[:], in0=o[:], in1=tanh_c[:])
-            nc.sync.dma_start(
-                out=out_0[b * P : (b + 1) * P, half * BLOCK_ROWS : (half + 1) * BLOCK_ROWS], in_=o[:]
-            )
-
+        sums = {}
         prepare(0)
         quantise_block(0)
         for n in range(len(blocks)):
             half, gate = blocks[n]
+            cols = slice(half * BLOCK_ROWS, (half + 1) * BLOCK_ROWS)
+            x_passes(n)
             if n + 1 < len(blocks):
                 prepare(n + 1)
-            for b in range(ROW_TILES):
-                gate_values(n, b)
-                if b == 0 and n + 1 < len(blocks):
-                    quantise_block(n + 1)
-                if gate == GATE_O and b >= 1:
-                    hidden_state(half, b - 1)
             if gate == GATE_O:
-                hidden_state(half, ROW_TILES - 1)
+                for b in range(ROW_TILES):
+                    nc.scalar.activation(out=gates[(GATE_G, b)][:], in_=gates[(GATE_F, b)][:], func=TANH)
+            for b in range(ROW_TILES):
+                h_passes(n, b)
+                if gate == GATE_F:
+                    f = gates[(GATE_F, b)]
+                    nc.gpsimd.tensor_mul(out=f[:], in0=f[:], in1=c_sb[:, b, cols])
+                if gate == GATE_G:
+                    i = gates[(GATE_I, b)]
+                    nc.gpsimd.tensor_mul(out=i[:], in0=i[:], in1=gates[(GATE_G, b)][:])
+            if n + 1 < len(blocks):
+                quantise_block(n + 1)
+            for b in range(ROW_TILES):
+                rows = slice(b * P, (b + 1) * P)
+                if gate == GATE_G:
+                    c_new = gates[(GATE_F, b)]
+                    nc.vector.tensor_add(out=c_new[:], in0=c_new[:], in1=gates[(GATE_I, b)][:])
+                    nc.sync.dma_start(out=out_1[rows, cols], in_=c_new[:])
+                if gate == GATE_O:
+                    hs = gates[(GATE_O, b)]
+                    nc.vector.tensor_mul(out=hs[:], in0=hs[:], in1=gates[(GATE_G, b)][:])
+                    nc.sync.dma_start(out=out_0[rows, cols], in_=hs[:])

@@ -27,21 +27,24 @@ PASS_WORDS = K_PASS // 2
 HALVES = HIDDEN // BLOCK_ROWS
 
 GATE_I, GATE_F, GATE_G, GATE_O = 0, 1, 2, 3
-GATE_ORDER = (GATE_F, GATE_I, GATE_G, GATE_O)
+WH_SCALAR_TILES = 3
+TANH_LAG = 2
 
 FLOPS = 2 * BATCH * 4 * HIDDEN * 2 * K
 
 
 def tile_lstmcell_e_kernel(tc, x, h, c, Wx_words, Wx_scales, Wh, bx, bh, out_0, out_1):
     nc = tc.nc
-    blocks = [(half, gate) for half in range(HALVES) for gate in GATE_ORDER]
+    blocks = [(half, gate) for half in range(HALVES) for gate in (GATE_F, GATE_I, GATE_G)]
+    blocks += [(half, GATE_O) for half in range(HALVES)]
 
     with ExitStack() as ctx:
         keep = ctx.enter_context(tc.tile_pool(name="keep", bufs=1))
-        grouped_pool = ctx.enter_context(tc.tile_pool(name="grouped", bufs=3))
-        wh_mx_pool = ctx.enter_context(tc.tile_pool(name="wh_mx", bufs=3))
-        bias_pool = ctx.enter_context(tc.tile_pool(name="bias", bufs=3))
-        gate_pool = ctx.enter_context(tc.tile_pool(name="gates", bufs=ROW_TILES))
+        raw_pool = ctx.enter_context(tc.tile_pool(name="raw", bufs=len(blocks) + 2))
+        grouped_pool = ctx.enter_context(tc.tile_pool(name="grouped", bufs=2))
+        wh_mx_pool = ctx.enter_context(tc.tile_pool(name="wh_mx", bufs=2))
+        bias_pool = ctx.enter_context(tc.tile_pool(name="bias", bufs=2))
+        gate_pool = ctx.enter_context(tc.tile_pool(name="gates", bufs=HALVES * ROW_TILES))
         flip_psum = ctx.enter_context(tc.psum_pool(name="flip", bufs=3))
         sum_psum = ctx.enter_context(tc.psum_pool(name="sums", bufs=ROW_TILES))
         spread_psum = ctx.enter_context(tc.psum_pool(name="spread", bufs=1))
@@ -59,13 +62,13 @@ def tile_lstmcell_e_kernel(tc, x, h, c, Wx_words, Wx_scales, Wh, bx, bh, out_0, 
         make_identity(nc, identity[:])
         nc.scalar.activation(out=warm[:], in_=warm[:], func=SIGMOID)
 
-        def load_rows(rows, label):
-            raw = keep.tile([P, ROW_TILES, K], BF16, name="raw_" + label, tag="raw_" + label)
+        def load_rows(rows):
+            raw = raw_pool.tile([P, ROW_TILES, K], BF16)
             nc.sync.dma_start(out=raw[:], in_=rows.rearrange("(r p) k -> p r k", p=P))
             return raw
 
-        x_raw = load_rows(x, "x")
-        h_raw = load_rows(h, "h")
+        x_raw = load_rows(x)
+        h_raw = load_rows(h)
         nc.gpsimd.dma_start(out=bias_rows[0:1, :], in_=bx.rearrange("(o g) n -> o (g n)", o=1))
         nc.gpsimd.dma_start(out=bias_rows[1:2, :], in_=bh.rearrange("(o g) n -> o (g n)", o=1))
 
@@ -74,23 +77,22 @@ def tile_lstmcell_e_kernel(tc, x, h, c, Wx_words, Wx_scales, Wh, bx, bh, out_0, 
         scales_dram = Wx_scales.bitcast(I32).rearrange("s (q r) n -> r q s n", r=4)
         c_sb = keep.tile([P, ROW_TILES, HIDDEN], BF16)
         wh_raw = []
-        for half in range(HALVES):
-            for gate in GATE_ORDER:
-                wh_rows = Wh[gate, half * BLOCK_ROWS : (half + 1) * BLOCK_ROWS, :]
-                wh_raw.append(load_rows(wh_rows, "wh%d%d" % (half, gate)))
-                if half == 0 and gate == GATE_ORDER[0]:
-                    for r in range(4):
-                        nc.sync.dma_start(out=wx_planes[r:P:32, :, :].bitcast(I32), in_=scales_dram[r])
-                if half == 0:
-                    first, last = gate * PASSES, (gate + 1) * PASSES
-                    nc.sync.dma_start(
-                        out=wx_words[:, first:last, :].bitcast(I32),
-                        in_=words_dram[first:last].rearrange("s p n -> p s n"),
-                    )
+        for n in range(len(blocks)):
+            half, gate = blocks[n]
+            wh_raw.append(load_rows(Wh[gate, half * BLOCK_ROWS : (half + 1) * BLOCK_ROWS, :]))
+            if n == 0:
+                for r in range(4):
+                    nc.sync.dma_start(out=wx_planes[r:P:32, :, :].bitcast(I32), in_=scales_dram[r])
             if half == 0:
+                first, last = gate * PASSES, (gate + 1) * PASSES
+                nc.sync.dma_start(
+                    out=wx_words[:, first:last, :].bitcast(I32),
+                    in_=words_dram[first:last].rearrange("s p n -> p s n"),
+                )
+            if n == 1:
                 nc.sync.dma_start(out=c_sb[:], in_=c.rearrange("(b p) n -> p b n", p=P))
 
-        def transpose_block(raw, k_step, copy_out):
+        def transpose_block(raw, k_step, scalar_tiles):
             grouped = grouped_pool.tile([P, PASSES, BLOCK_ROWS, PACK], BF16, align_bytes=64)
             for r in range(ROW_TILES):
                 words = raw[:, r, :].bitcast(F32)
@@ -102,6 +104,7 @@ def tile_lstmcell_e_kernel(tc, x, h, c, Wx_words, Wx_scales, Wh, bx, bh, out_0, 
                         else:
                             cols = words[:, s * PASS_WORDS + u * P : s * PASS_WORDS + (u + 1) * P]
                         nc.tensor.transpose(flipped[:, s, u, :], cols, identity[:])
+                copy_out = nc.scalar.copy if r < scalar_tiles else nc.vector.tensor_copy
                 copy_out(
                     out=grouped[:, :, r * P : (r + 1) * P, :].bitcast(F32),
                     in_=flipped[:].rearrange("p s u n -> p s n u"),
@@ -119,8 +122,8 @@ def tile_lstmcell_e_kernel(tc, x, h, c, Wx_words, Wx_scales, Wh, bx, bh, out_0, 
         x_planes = keep.tile([P, PASSES, BATCH], U8, align_bytes=64)
         h_codes = keep.tile([P, PASSES, BATCH], U32, align_bytes=64)
         h_planes = keep.tile([P, PASSES, BATCH], U8, align_bytes=64)
-        x_grouped = transpose_block(x_raw, 2, nc.vector.tensor_copy)
-        h_grouped = transpose_block(h_raw, 1, nc.vector.tensor_copy)
+        x_grouped = transpose_block(x_raw, 2, 0)
+        h_grouped = transpose_block(h_raw, 1, 0)
         quantise(x_grouped, x_codes, x_planes)
         quantise(h_grouped, h_codes, h_planes)
 
@@ -131,14 +134,14 @@ def tile_lstmcell_e_kernel(tc, x, h, c, Wx_words, Wx_scales, Wh, bx, bh, out_0, 
 
         def prepare(n):
             half, gate = blocks[n]
-            wh_grouped[n] = transpose_block(wh_raw[n], 1, nc.scalar.copy)
+            wh_grouped[n] = transpose_block(wh_raw[n], 1, WH_SCALAR_TILES)
             start_col = gate * HIDDEN + half * BLOCK_ROWS
             spread = spread_psum.tile([P, BLOCK_ROWS], F32)
             nc.tensor.matmul(
                 spread[:], lhsT=ones[:], rhs=bias_rows[:, start_col : start_col + BLOCK_ROWS], start=True, stop=True
             )
             bias[n] = bias_pool.tile([P, BLOCK_ROWS], F32, name="bias_sb")
-            nc.scalar.copy(out=bias[n][:], in_=spread[:])
+            nc.vector.tensor_copy(out=bias[n][:], in_=spread[:])
 
         def quantise_block(n):
             codes = wh_mx_pool.tile([P, PASSES, BLOCK_ROWS], U32, name="wh_codes", align_bytes=64)
@@ -179,7 +182,7 @@ def tile_lstmcell_e_kernel(tc, x, h, c, Wx_words, Wx_scales, Wh, bx, bh, out_0, 
             value = gate_pool.tile([P, BLOCK_ROWS], F32, name="gate%d" % gate, tag="gate%d" % gate)
             nc.vector.tensor_add(out=value[:], in0=sums[b][:], in1=bias[n][:])
             nc.scalar.activation(out=value[:], in_=value[:], func=(TANH if gate == GATE_G else SIGMOID))
-            gates[(gate, b)] = value
+            gates[(gate, half, b)] = value
 
         sums = {}
         prepare(0)
@@ -190,26 +193,25 @@ def tile_lstmcell_e_kernel(tc, x, h, c, Wx_words, Wx_scales, Wh, bx, bh, out_0, 
             x_passes(n)
             if n + 1 < len(blocks):
                 prepare(n + 1)
-            if gate == GATE_O:
+            if n >= TANH_LAG and blocks[n - TANH_LAG][1] == GATE_G:
                 for b in range(ROW_TILES):
-                    nc.scalar.activation(out=gates[(GATE_G, b)][:], in_=gates[(GATE_F, b)][:], func=TANH)
+                    earlier = blocks[n - TANH_LAG][0]
+                    nc.scalar.activation(
+                        out=gates[(GATE_G, earlier, b)][:], in_=gates[(GATE_F, earlier, b)][:], func=TANH
+                    )
             for b in range(ROW_TILES):
                 h_passes(n, b)
+                f, i, g = [gates.get((e, half, b)) for e in (GATE_F, GATE_I, GATE_G)]
                 if gate == GATE_F:
-                    f = gates[(GATE_F, b)]
                     nc.gpsimd.tensor_mul(out=f[:], in0=f[:], in1=c_sb[:, b, cols])
                 if gate == GATE_G:
-                    i = gates[(GATE_I, b)]
-                    nc.gpsimd.tensor_mul(out=i[:], in0=i[:], in1=gates[(GATE_G, b)][:])
+                    nc.gpsimd.tensor_mul(out=i[:], in0=i[:], in1=g[:])
+                    nc.gpsimd.tensor_add(out=f[:], in0=f[:], in1=i[:])
+                    nc.sync.dma_start(out=out_1[b * P : (b + 1) * P, cols], in_=f[:])
             if n + 1 < len(blocks):
                 quantise_block(n + 1)
-            for b in range(ROW_TILES):
-                rows = slice(b * P, (b + 1) * P)
-                if gate == GATE_G:
-                    c_new = gates[(GATE_F, b)]
-                    nc.vector.tensor_add(out=c_new[:], in0=c_new[:], in1=gates[(GATE_I, b)][:])
-                    nc.sync.dma_start(out=out_1[rows, cols], in_=c_new[:])
-                if gate == GATE_O:
-                    hs = gates[(GATE_O, b)]
-                    nc.vector.tensor_mul(out=hs[:], in0=hs[:], in1=gates[(GATE_G, b)][:])
-                    nc.sync.dma_start(out=out_0[rows, cols], in_=hs[:])
+            if gate == GATE_O:
+                for b in range(ROW_TILES):
+                    hs = gates[(GATE_O, half, b)]
+                    nc.vector.tensor_mul(out=hs[:], in0=hs[:], in1=gates[(GATE_G, half, b)][:])
+                    nc.sync.dma_start(out=out_0[b * P : (b + 1) * P, cols], in_=hs[:])

@@ -89,7 +89,7 @@ def tile_lstmcell_e_kernel(tc, x, h, c, Wx_words, Wx_scales, Wh, bx, bh, out_0, 
                     out=wx_words[:, first:last, :].bitcast(I32),
                     in_=words_dram[first:last].rearrange("s p n -> p s n"),
                 )
-            if n == 1:
+            if n == 2:
                 nc.sync.dma_start(out=c_sb[:], in_=c.rearrange("(b p) n -> p b n", p=P))
 
         def transpose_block(raw, k_step, scalar_tiles):
@@ -122,8 +122,8 @@ def tile_lstmcell_e_kernel(tc, x, h, c, Wx_words, Wx_scales, Wh, bx, bh, out_0, 
         x_planes = keep.tile([P, PASSES, BATCH], U8, align_bytes=64)
         h_codes = keep.tile([P, PASSES, BATCH], U32, align_bytes=64)
         h_planes = keep.tile([P, PASSES, BATCH], U8, align_bytes=64)
-        x_grouped = transpose_block(x_raw, 2, 0)
-        h_grouped = transpose_block(h_raw, 1, 0)
+        x_grouped = transpose_block(x_raw, 2, ROW_TILES // 2)
+        h_grouped = transpose_block(h_raw, 1, ROW_TILES // 2)
         quantise(x_grouped, x_codes, x_planes)
         quantise(h_grouped, h_codes, h_planes)
 
@@ -141,7 +141,7 @@ def tile_lstmcell_e_kernel(tc, x, h, c, Wx_words, Wx_scales, Wh, bx, bh, out_0, 
                 spread[:], lhsT=ones[:], rhs=bias_rows[:, start_col : start_col + BLOCK_ROWS], start=True, stop=True
             )
             bias[n] = bias_pool.tile([P, BLOCK_ROWS], F32, name="bias_sb")
-            nc.vector.tensor_copy(out=bias[n][:], in_=spread[:])
+            nc.scalar.copy(out=bias[n][:], in_=spread[:])
 
         def quantise_block(n):
             codes = wh_mx_pool.tile([P, PASSES, BLOCK_ROWS], U32, name="wh_codes", align_bytes=64)
@@ -211,7 +211,8 @@ def tile_lstmcell_e_kernel(tc, x, h, c, Wx_words, Wx_scales, Wh, bx, bh, out_0, 
             if n + 1 < len(blocks):
                 quantise_block(n + 1)
             if gate == GATE_O:
+                multiply = nc.vector.tensor_mul if n == len(blocks) - 1 else nc.gpsimd.tensor_mul
                 for b in range(ROW_TILES):
                     hs = gates[(GATE_O, half, b)]
-                    nc.vector.tensor_mul(out=hs[:], in0=hs[:], in1=gates[(GATE_G, half, b)][:])
+                    multiply(out=hs[:], in0=hs[:], in1=gates[(GATE_G, half, b)][:])
                     nc.sync.dma_start(out=out_0[b * P : (b + 1) * P, cols], in_=hs[:])

@@ -45,9 +45,8 @@ def tile_lstmcell_e_kernel(tc, x, h, c, Wx_words, Wx_scales, Wh, bx, bh, out_0, 
         wh_mx_pool = ctx.enter_context(tc.tile_pool(name="wh_mx", bufs=2))
         bias_pool = ctx.enter_context(tc.tile_pool(name="bias", bufs=2))
         gate_pool = ctx.enter_context(tc.tile_pool(name="gates", bufs=HALVES * ROW_TILES))
-        flip_psum = ctx.enter_context(tc.psum_pool(name="flip", bufs=3))
+        flip_psum = ctx.enter_context(tc.psum_pool(name="flip", bufs=ROW_TILES))
         sum_psum = ctx.enter_context(tc.psum_pool(name="sums", bufs=ROW_TILES))
-        spread_psum = ctx.enter_context(tc.psum_pool(name="spread", bufs=1))
         ctx.enter_context(tc.manual_schedule())
 
         wx_planes = keep.tile([P, 4 * PASSES, HIDDEN], U8, align_bytes=64)
@@ -89,7 +88,7 @@ def tile_lstmcell_e_kernel(tc, x, h, c, Wx_words, Wx_scales, Wh, bx, bh, out_0, 
                     out=wx_words[:, first:last, :].bitcast(I32),
                     in_=words_dram[first:last].rearrange("s p n -> p s n"),
                 )
-            if n == 2:
+            if n == 1:
                 nc.sync.dma_start(out=c_sb[:], in_=c.rearrange("(b p) n -> p b n", p=P))
 
         def transpose_block(raw, k_step, scalar_tiles):
@@ -122,8 +121,8 @@ def tile_lstmcell_e_kernel(tc, x, h, c, Wx_words, Wx_scales, Wh, bx, bh, out_0, 
         x_planes = keep.tile([P, PASSES, BATCH], U8, align_bytes=64)
         h_codes = keep.tile([P, PASSES, BATCH], U32, align_bytes=64)
         h_planes = keep.tile([P, PASSES, BATCH], U8, align_bytes=64)
-        x_grouped = transpose_block(x_raw, 2, ROW_TILES // 2)
-        h_grouped = transpose_block(h_raw, 1, ROW_TILES // 2)
+        x_grouped = transpose_block(x_raw, 2, 0)
+        h_grouped = transpose_block(h_raw, 1, 0)
         quantise(x_grouped, x_codes, x_planes)
         quantise(h_grouped, h_codes, h_planes)
 
@@ -136,12 +135,12 @@ def tile_lstmcell_e_kernel(tc, x, h, c, Wx_words, Wx_scales, Wh, bx, bh, out_0, 
             half, gate = blocks[n]
             wh_grouped[n] = transpose_block(wh_raw[n], 1, WH_SCALAR_TILES)
             start_col = gate * HIDDEN + half * BLOCK_ROWS
-            spread = spread_psum.tile([P, BLOCK_ROWS], F32)
+            spread = flip_psum.tile([P, BLOCK_ROWS], F32, tag="bank")
             nc.tensor.matmul(
                 spread[:], lhsT=ones[:], rhs=bias_rows[:, start_col : start_col + BLOCK_ROWS], start=True, stop=True
             )
             bias[n] = bias_pool.tile([P, BLOCK_ROWS], F32, name="bias_sb")
-            nc.scalar.copy(out=bias[n][:], in_=spread[:])
+            nc.vector.tensor_copy(out=bias[n][:], in_=spread[:])
 
         def quantise_block(n):
             codes = wh_mx_pool.tile([P, PASSES, BLOCK_ROWS], U32, name="wh_codes", align_bytes=64)
@@ -211,8 +210,7 @@ def tile_lstmcell_e_kernel(tc, x, h, c, Wx_words, Wx_scales, Wh, bx, bh, out_0, 
             if n + 1 < len(blocks):
                 quantise_block(n + 1)
             if gate == GATE_O:
-                multiply = nc.vector.tensor_mul if n == len(blocks) - 1 else nc.gpsimd.tensor_mul
                 for b in range(ROW_TILES):
                     hs = gates[(GATE_O, half, b)]
-                    multiply(out=hs[:], in0=hs[:], in1=gates[(GATE_G, half, b)][:])
+                    nc.vector.tensor_mul(out=hs[:], in0=hs[:], in1=gates[(GATE_G, half, b)][:])
                     nc.sync.dma_start(out=out_0[b * P : (b + 1) * P, cols], in_=hs[:])

from contextlib import ExitStack

import concourse.mybir as mybir
from concourse.masks import make_identity

F32 = mybir.dt.float32
BF16 = mybir.dt.bfloat16
I32 = mybir.dt.int32
U32 = mybir.dt.uint32
U8 = mybir.dt.uint8
FP8X4 = mybir.dt.float8_e4m3fn_x4
FP4X4 = mybir.dt.float4_e2m1fn_x4
SIGMOID = mybir.ActivationFunctionType.Sigmoid
TANH = mybir.ActivationFunctionType.Tanh

P = 128
PACK = 4
K_PASS = P * PACK
BATCH = 512
K = 1024
HIDDEN = 1024
PASSES = K // K_PASS
BLOCK_ROWS = 512
ROW_TILES = BLOCK_ROWS // P
WORDS = K // 2
PASS_WORDS = K_PASS // 2
HALVES = HIDDEN // BLOCK_ROWS

GATE_I, GATE_F, GATE_G, GATE_O = 0, 1, 2, 3
WH_SCALAR_TILES = 3
TANH_LAG = 2

FLOPS = 2 * BATCH * 4 * HIDDEN * 2 * K


def tile_lstmcell_e_kernel(tc, x, h, c, Wx_words, Wx_scales, Wh, bx, bh, out_0, out_1):
    nc = tc.nc
    blocks = [(half, gate) for half in range(HALVES) for gate in (GATE_F, GATE_I, GATE_G)]
    blocks += [(half, GATE_O) for half in range(HALVES)]

    with ExitStack() as ctx:
        keep = ctx.enter_context(tc.tile_pool(name="keep", bufs=1))
        raw_pool = ctx.enter_context(tc.tile_pool(name="raw", bufs=len(blocks) + 2))
        grouped_pool = ctx.enter_context(tc.tile_pool(name="grouped", bufs=2))
        wh_mx_pool = ctx.enter_context(tc.tile_pool(name="wh_mx", bufs=2))
        bias_pool = ctx.enter_context(tc.tile_pool(name="bias", bufs=2))
        gate_pool = ctx.enter_context(tc.tile_pool(name="gates", bufs=HALVES * ROW_TILES))
        flip_psum = ctx.enter_context(tc.psum_pool(name="flip", bufs=ROW_TILES))
        sum_psum = ctx.enter_context(tc.psum_pool(name="sums", bufs=ROW_TILES))
        ctx.enter_context(tc.manual_schedule())

        wx_planes = keep.tile([P, 4 * PASSES, HIDDEN], U8, align_bytes=64)
        nc.vector.memset(wx_planes[:].rearrange("p s n -> p (s n)").bitcast(I32), 0)
        bias_rows = keep.tile([P, 4 * HIDDEN], BF16)
        nc.vector.memset(bias_rows[:].bitcast(I32), 0)
        ones = keep.tile([P, P], BF16)
        nc.vector.memset(ones[:], 1.0)
        warm = keep.tile([P, 1], F32)
        nc.vector.memset(warm[:], 0.0)
        identity = keep.tile([P, P], F32)
        make_identity(nc, identity[:])
        nc.scalar.activation(out=warm[:], in_=warm[:], func=SIGMOID)

        def load_rows(rows):
            raw = raw_pool.tile([P, ROW_TILES, K], BF16)
            nc.sync.dma_start(out=raw[:], in_=rows.rearrange("(r p) k -> p r k", p=P))
            return raw

        x_raw = load_rows(x)
        h_raw = load_rows(h)
        nc.gpsimd.dma_start(out=bias_rows[0:1, :], in_=bx.rearrange("(o g) n -> o (g n)", o=1))
        nc.gpsimd.dma_start(out=bias_rows[1:2, :], in_=bh.rearrange("(o g) n -> o (g n)", o=1))

        wx_words = keep.tile([P, 4 * PASSES, 2 * HIDDEN], U8, align_bytes=64)
        words_dram = Wx_words.bitcast(I32)
        scales_dram = Wx_scales.bitcast(I32).rearrange("s (q r) n -> r q s n", r=4)
        c_sb = keep.tile([P, ROW_TILES, HIDDEN], BF16)
        wh_raw = []
        for n in range(len(blocks)):
            half, gate = blocks[n]
            wh_raw.append(load_rows(Wh[gate, half * BLOCK_ROWS : (half + 1) * BLOCK_ROWS, :]))
            if n == 0:
                for r in range(4):
                    nc.sync.dma_start(out=wx_planes[r:P:32, :, :].bitcast(I32), in_=scales_dram[r])
            if half == 0:
                first, last = gate * PASSES, (gate + 1) * PASSES
                nc.sync.dma_start(
                    out=wx_words[:, first:last, :].bitcast(I32),
                    in_=words_dram[first:last].rearrange("s p n -> p s n"),
                )
            if n == 1:
                nc.sync.dma_start(out=c_sb[:], in_=c.rearrange("(b p) n -> p b n", p=P))

        def transpose_block(raw, k_step, scalar_tiles):
            grouped = grouped_pool.tile([P, PASSES, BLOCK_ROWS, PACK], BF16, align_bytes=64)
            for r in range(ROW_TILES):
                words = raw[:, r, :].bitcast(F32)
                flipped = flip_psum.tile([P, PASSES, 2, P], F32, tag="bank")
                for s in range(PASSES):
                    for u in range(2):
                        if k_step == 2:
                            cols = words[:, s * PASS_WORDS + u : (s + 1) * PASS_WORDS : 2]
                        else:
                            cols = words[:, s * PASS_WORDS + u * P : s * PASS_WORDS + (u + 1) * P]
                        nc.tensor.transpose(flipped[:, s, u, :], cols, identity[:])
                copy_out = nc.scalar.copy if r < scalar_tiles else nc.vector.tensor_copy
                copy_out(
                    out=grouped[:, :, r * P : (r + 1) * P, :].bitcast(F32),
                    in_=flipped[:].rearrange("p s u n -> p s n u"),
                )
            return grouped

        def quantise(grouped, codes, planes):
            nc.vector.quantize_mx(
                out=codes[:].rearrange("p s n -> p (s n)").bitcast(FP8X4),
                scales=planes[:].rearrange("p s n -> p (s n)"),
                in_=grouped[:].rearrange("p s n t -> p (s n t)"),
            )

        x_codes = keep.tile([P, PASSES, BATCH], U32, align_bytes=64)
        x_planes = keep.tile([P, PASSES, BATCH], U8, align_bytes=64)
        h_codes = keep.tile([P, PASSES, BATCH], U32, align_bytes=64)
        h_planes = keep.tile([P, PASSES, BATCH], U8, align_bytes=64)
        x_grouped = transpose_block(x_raw, 2, 0)
        h_grouped = transpose_block(h_raw, 1, 0)
        quantise(x_grouped, x_codes, x_planes)
        quantise(h_grouped, h_codes, h_planes)

        wh_grouped = {}
        wh_mx = {}
        bias = {}
        gates = {}

        def prepare(n):
            half, gate = blocks[n]
            wh_grouped[n] = transpose_block(wh_raw[n], 1, WH_SCALAR_TILES)
            start_col = gate * HIDDEN + half * BLOCK_ROWS
            spread = flip_psum.tile([P, BLOCK_ROWS], F32, tag="bank")
            nc.tensor.matmul(
                spread[:], lhsT=ones[:], rhs=bias_rows[:, start_col : start_col + BLOCK_ROWS], start=True, stop=True
            )
            bias[n] = bias_pool.tile([P, BLOCK_ROWS], F32, name="bias_sb")
            nc.vector.tensor_copy(out=bias[n][:], in_=spread[:])

        def quantise_block(n):
            codes = wh_mx_pool.tile([P, PASSES, BLOCK_ROWS], U32, name="wh_codes", align_bytes=64)
            planes = wh_mx_pool.tile([P, PASSES, BLOCK_ROWS], U8, name="wh_planes", align_bytes=64)
            quantise(wh_grouped[n], codes, planes)
            wh_mx[n] = (codes, planes)

        def x_passes(n):
            half, gate = blocks[n]
            for b in range(ROW_TILES):
                sums[b] = sum_psum.tile([P, BLOCK_ROWS], F32, name="acc")
                for s in range(PASSES):
                    nc.tensor.matmul_mx(
                        out=sums[b][:],
                        lhsT=x_codes[:, s, b * P : (b + 1) * P].bitcast(FP8X4),
                        lhsT_scale=x_planes[:, s, b * P : (b + 1) * P],
                        rhs=wx_words[
                            :, gate * PASSES + s, 2 * half * BLOCK_ROWS : 2 * (half + 1) * BLOCK_ROWS
                        ].bitcast(FP4X4),
                        rhs_scale=wx_planes[:, gate * PASSES + s, half * BLOCK_ROWS : (half + 1) * BLOCK_ROWS],
                        start=(s == 0),
                        stop=False,
                    )

        def h_passes(n, b):
            half, gate = blocks[n]
            wh_codes, wh_planes = wh_mx[n]
            for s in range(PASSES):
                nc.tensor.matmul_mx(
                    out=sums[b][:],
                    lhsT=h_codes[:, s, b * P : (b + 1) * P].bitcast(FP8X4),
                    lhsT_scale=h_planes[:, s, b * P : (b + 1) * P],
                    rhs=wh_codes[:, s, :].bitcast(FP8X4),
                    rhs_scale=wh_planes[:, s, :],
                    start=False,
                    stop=(s == PASSES - 1),
                )
            value = gate_pool.tile([P, BLOCK_ROWS], F32, name="gate%d" % gate, tag="gate%d" % gate)
            nc.vector.tensor_add(out=value[:], in0=sums[b][:], in1=bias[n][:])
            nc.scalar.activation(out=value[:], in_=value[:], func=(TANH if gate == GATE_G else SIGMOID))
            gates[(gate, half, b)] = value

        sums = {}
        prepare(0)
        quantise_block(0)
        for n in range(len(blocks)):
            half, gate = blocks[n]
            cols = slice(half * BLOCK_ROWS, (half + 1) * BLOCK_ROWS)
            x_passes(n)
            if n + 1 < len(blocks):
                prepare(n + 1)
            if n >= TANH_LAG and blocks[n - TANH_LAG][1] == GATE_G:
                for b in range(ROW_TILES):
                    earlier = blocks[n - TANH_LAG][0]
                    nc.scalar.activation(
                        out=gates[(GATE_G, earlier, b)][:], in_=gates[(GATE_F, earlier, b)][:], func=TANH
                    )
            for b in range(ROW_TILES):
                h_passes(n, b)
                f, i, g = [gates.get((e, half, b)) for e in (GATE_F, GATE_I, GATE_G)]
                if gate == GATE_F:
                    nc.gpsimd.tensor_mul(out=f[:], in0=f[:], in1=c_sb[:, b, cols])
                if gate == GATE_G:
                    nc.gpsimd.tensor_mul(out=i[:], in0=i[:], in1=g[:])
                    nc.gpsimd.tensor_add(out=f[:], in0=f[:], in1=i[:])
                    nc.sync.dma_start(out=out_1[b * P : (b + 1) * P, cols], in_=f[:])
            if n + 1 < len(blocks):
                quantise_block(n + 1)
            if gate == GATE_O:
                for b in range(ROW_TILES):
                    hs = gates[(GATE_O, half, b)]
                    nc.vector.tensor_mul(out=hs[:], in0=hs[:], in1=gates[(GATE_G, half, b)][:])
                    nc.sync.dma_start(out=out_0[b * P : (b + 1) * P, cols], in_=hs[:])
